import numpy as np
import ml_dtypes


def mxq(x, axis, fmt="e4m3"):
    dtype, down = {"e4m3": (ml_dtypes.float8_e4m3fn, 7), "e5m2": (ml_dtypes.float8_e5m2, 14)}[fmt]
    v = np.moveaxis(np.asarray(x, np.float32).astype(ml_dtypes.bfloat16).astype(np.float64), axis, -1)
    blocks = v.reshape(v.shape[:-1] + (-1, 32))
    amax = np.abs(blocks).max(-1, keepdims=True)
    byte = np.maximum(np.where(amax > 0, np.frexp(amax)[1] - 1 + 127, 0) - down, 1)
    scale = np.exp2(byte - 127.0)
    codes = (blocks / scale).astype(np.float32).astype(dtype).astype(np.float64)
    return np.moveaxis((codes * scale).reshape(v.shape), -1, axis)


WIDE = False


def mx_kscale(k):
    if not WIDE:
        return np.ones(k)
    levels = np.array([10, -10, 5, -5, 0])
    a = np.random.permutation(np.resize(levels, k // 512 * 4)).reshape(k // 512, 4)
    idx = np.arange(k)
    return np.exp2(a[idx // 512, idx % 128 // 32])


BF16 = ml_dtypes.bfloat16


def bf(x):
    return np.asarray(x, np.float32).astype(BF16)


def f64(x):
    return np.asarray(x).astype(np.float64)


E2M1 = np.array([0.0, 0.5, 1.0, 1.5, 2.0, 3.0, 4.0, 6.0, -0.0, -0.5, -1.0, -1.5, -2.0, -3.0, -4.0, -6.0])


def pack_weight(w, fmt):
    k, n = w.shape
    w = f64(bf(w)).reshape(k // 32, 32, n)
    amax = np.abs(w).max(1)
    if fmt == "e4m3":
        byte = np.frexp(amax)[1] - 1 + 127 - 7
    else:
        mant, ex = np.frexp(amax / 6.0)
        byte = np.where(mant > 0.5, ex, ex - 1) + 127
    byte = np.clip(np.where(amax > 0, byte, 1), 1, 254)
    scaled = (w * np.exp2(127.0 - byte)[:, None, :]).reshape(k, n).astype(np.float32)
    by_word = np.ascontiguousarray(scaled.reshape(k // 512, 128, 4, n).transpose(0, 1, 3, 2))
    if fmt == "e4m3":
        words = by_word.astype(ml_dtypes.float8_e4m3fn).view(np.uint8)
    else:
        c = by_word.astype(ml_dtypes.float4_e2m1fn).view(np.uint8) & 0xF
        words = c[..., 0::2] | (c[..., 1::2] << 4)
    return np.ascontiguousarray(words), np.ascontiguousarray(byte.astype(np.uint8).reshape(k // 512, 16, n))


def unpack_weight(words, scales, fmt):
    g, p, n, _ = words.shape
    if fmt == "e4m3":
        vals = np.ascontiguousarray(words).view(ml_dtypes.float8_e4m3fn).astype(np.float64)
    else:
        nib = np.empty((g, p, n, 4), np.uint8)
        nib[..., 0::2] = words & 0xF
        nib[..., 1::2] = words >> 4
        vals = E2M1[nib]
    vals = vals * np.repeat(np.exp2(scales.astype(np.float64) - 127.0), 8, axis=1)[..., None]
    return vals.transpose(0, 1, 3, 2).reshape(g * 512, n)


N, E, C = 512, 16384, 512
DENSITY = 0.01
HE_RMS = np.sqrt(np.e / E)


def setup_inputs():
    s, t = mx_kscale(E), mx_kscale(C)
    member = np.random.uniform(size=(N, E)) < DENSITY
    incidence = bf(member * s[None, :])
    he = bf(np.random.standard_normal((E, C)) * HE_RMS / s[:, None] * t[None, :])
    W2_words, W2_scales = pack_weight(np.random.standard_normal((C, C)) * 3.0 / np.sqrt(C) / t[:, None], "e4m3")
    return {"incidence": incidence,
            "he": he,
            "W2_words": W2_words,
            "W2_scales": W2_scales,
            "b2": bf(np.random.standard_normal(C) * 0.2),
            "node_features": bf(np.random.standard_normal((N, C)))}


def reference(incidence, he, W2_words, W2_scales, b2, node_features):
    prop = mxq(f64(incidence), 1, "e4m3") @ mxq(f64(he), 0, "e4m3")
    return (mxq(prop, 1, "e4m3") @ unpack_weight(W2_words, W2_scales, "e4m3")) + f64(b2) + f64(node_features)

@@ -1,0 +1,198 @@
+from contextlib import ExitStack
+
+import concourse.mybir as mybir
+from concourse.masks import make_identity
+
+F32 = mybir.dt.float32
+BF16 = mybir.dt.bfloat16
+I32 = mybir.dt.int32
+U32 = mybir.dt.uint32
+U8 = mybir.dt.uint8
+FP8X4 = mybir.dt.float8_e4m3fn_x4
+ADD = mybir.AluOpType.add
+
+P = 128
+PACK = 4
+K_PASS = P * PACK
+
+NODES = 512
+EDGES = 16384
+CHANNELS = 512
+NODE_TILES = NODES // P
+PASSES = EDGES // K_PASS
+
+CHUNK_PASSES = 4
+CHUNK_EDGES = CHUNK_PASSES * K_PASS
+INC_BUFS = 3
+HE_BUFS = 6
+
+HE_COLS = PACK * CHANNELS
+INC_COLS = PACK * NODES
+BANK_WORDS = 512
+VECTOR_WORDS = 80
+
+FLOPS = 2 * NODES * EDGES * CHANNELS + 2 * NODES * CHANNELS * CHANNELS
+
+
+def tile_heterogeneoustemporalhypergraphnn_pb_k_kernel(
+    tc, incidence, he, W2_words, W2_scales, b2, node_features, out
+):
+    nc = tc.nc
+    with ExitStack() as ctx:
+        consts = ctx.enter_context(tc.tile_pool(name="consts", bufs=1))
+        inc_pool = ctx.enter_context(tc.tile_pool(name="inc", bufs=INC_BUFS))
+        he_pool = ctx.enter_context(tc.tile_pool(name="he", bufs=HE_BUFS))
+        grouped_pool = ctx.enter_context(tc.tile_pool(name="grouped", bufs=4))
+        mx_pool = ctx.enter_context(tc.tile_pool(name="mx", bufs=3))
+        out_pool = ctx.enter_context(tc.tile_pool(name="out", bufs=NODE_TILES))
+        acc_pool = ctx.enter_context(tc.psum_pool(name="acc", bufs=1))
+        bank_pool = ctx.enter_context(tc.psum_pool(name="bank", bufs=4))
+        ctx.enter_context(tc.manual_schedule())
+
+        identity = consts.tile([P, P], F32)
+        make_identity(nc, identity[:])
+
+        features = consts.tile([P, NODE_TILES, CHANNELS], BF16)
+        nc.sync.dma_start(out=features[:], in_=node_features.rearrange("(a p) c -> p a c", p=P))
+
+        w2_codes = consts.tile([P, CHANNELS], U32, align_bytes=64)
+        nc.sync.dma_start(
+            out=w2_codes[:].bitcast(I32),
+            in_=W2_words[0].rearrange("p n t -> p (n t)").bitcast(I32),
+        )
+
+        ones = consts.tile([P, P], BF16)
+        nc.vector.memset(ones[:], 1.0)
+        bias_rows = consts.tile([P, CHANNELS], BF16)
+        nc.vector.memset(bias_rows[:], 0.0)
+        nc.sync.dma_start(out=bias_rows[0:1, :], in_=b2.unsqueeze(0))
+
+        w2_scales = consts.tile([P, CHANNELS], U8, align_bytes=64)
+        nc.vector.memset(w2_scales[:].bitcast(I32), 0)
+        for quadrant in range(4):
+            nc.sync.dma_start(
+                out=w2_scales[32 * quadrant : 32 * quadrant + 4, :].bitcast(I32),
+                in_=W2_scales[0, 4 * quadrant : 4 * quadrant + 4, :].bitcast(I32),
+            )
+
+        bias_bank = bank_pool.tile([P, CHANNELS], F32, name="bias_bank", tag="bank")
+        nc.tensor.matmul(out=bias_bank[:], lhsT=ones[:], rhs=bias_rows[:], start=True, stop=True)
+        residual = consts.tile([P, NODE_TILES, CHANNELS], F32)
+        for a in range(NODE_TILES):
+            nc.vector.tensor_tensor(out=residual[:, a, :], in0=bias_bank[:], in1=features[:, a, :], op=ADD)
+
+        acc = [acc_pool.tile([P, NODES], F32, name="acc%d" % t) for t in range(PACK)]
+
+        incidence_by_tile = incidence.rearrange("(a p) k -> p a k", p=P)
+        inc_raw = {}
+        he_raw = {}
+        grouped = {}
+        codes = {}
+        scales = {}
+
+        def load_incidence(chunk):
+            inc_raw[chunk] = inc_pool.tile([P, NODE_TILES, CHUNK_EDGES], BF16, name="inc_raw")
+            nc.sync.dma_start(
+                out=inc_raw[chunk][:],
+                in_=incidence_by_tile[:, :, chunk * CHUNK_EDGES : (chunk + 1) * CHUNK_EDGES],
+            )
+
+        def load_he(g):
+            he_raw[g] = he_pool.tile([P, PACK, CHANNELS], BF16, name="he_raw")
+            nc.sync.dma_start(
+                out=he_raw[g][:].rearrange("p (u e) c -> p u (e c)", u=2),
+                in_=he[g * K_PASS : (g + 1) * K_PASS, :].rearrange("(u p e) c -> p u (e c)", u=2, p=P),
+            )
+
+        def load_for(g):
+            if (g + 1) % CHUNK_PASSES == 0 and g + 1 < PASSES:
+                load_incidence((g + 1) // CHUNK_PASSES)
+            load_he(g)
+
+        def transpose_incidence(g):
+            grouped[g] = grouped_pool.tile([P, HE_COLS + INC_COLS], BF16, name="grouped", align_bytes=64)
+            words = inc_raw[g // CHUNK_PASSES][:].bitcast(F32)
+            first = (g % CHUNK_PASSES) * (K_PASS // 2)
+            inc_words = grouped[g][:, HE_COLS:].bitcast(F32)
+            for half in range(2):
+                bank = bank_pool.tile([P, 2, 2 * P], F32, name="xt", tag="bank")
+                for a in range(2):
+                    for u in range(2):
+                        nc.tensor.transpose(
+                            out=bank[:, u, a * P : (a + 1) * P],
+                            in_=words[:, 2 * half + a, first + u * P : first + (u + 1) * P],
+                            identity=identity[:],
+                        )
+                nc.scalar.copy(
+                    out=inc_words[:, half * BANK_WORDS : (half + 1) * BANK_WORDS].rearrange("p (n u) -> p n u", u=2),
+                    in_=bank[:].rearrange("p u n -> p n u"),
+                )
+
+        def regroup_he(g):
+            src = he_raw[g][:].rearrange("q j (p t) -> q p j t", t=PACK)
+            dst = grouped[g][:, 0:HE_COLS].rearrange("q (t p j) -> q p j t", t=PACK, j=PACK)
+            nc.vector.tensor_copy(out=dst[:, 0:VECTOR_WORDS], in_=src[:, 0:VECTOR_WORDS])
+            nc.scalar.copy(out=dst[:, VECTOR_WORDS:P], in_=src[:, VECTOR_WORDS:P])
+
+        def quantise(g):
+            codes[g] = mx_pool.tile([P, CHANNELS + NODES], U32, name="codes", align_bytes=64)
+            scales[g] = mx_pool.tile([P, CHANNELS + NODES], U8, name="scales", align_bytes=64)
+            nc.vector.quantize_mx(out=codes[g][:].bitcast(FP8X4), scales=scales[g][:], in_=grouped[g][:])
+
+        def multiply(g):
+            for t in range(PACK):
+                nc.tensor.matmul_mx(
+                    out=acc[t][:],
+                    lhsT=codes[g][:, t * P : (t + 1) * P].bitcast(FP8X4),
+                    lhsT_scale=scales[g][:, t * P : (t + 1) * P],
+                    rhs=codes[g][:, CHANNELS:].bitcast(FP8X4),
+                    rhs_scale=scales[g][:, CHANNELS:],
+                    start=(g == 0),
+                    stop=(g == PASSES - 1),
+                )
+
+        load_incidence(0)
+        for g in range(HE_BUFS):
+            load_for(g)
+
+        for step in range(-1, PASSES + 2):
+            if 0 <= step + 1 < PASSES:
+                transpose_incidence(step + 1)
+            if 0 <= step < PASSES:
+                regroup_he(step)
+            if 0 <= step - 1 < PASSES:
+                quantise(step - 1)
+            if 0 <= step - 2 < PASSES:
+                multiply(step - 2)
+            if 0 <= step and step + HE_BUFS < PASSES:
+                load_for(step + HE_BUFS)
+
+        prop_bf = consts.tile([P, PACK, NODES], BF16)
+        for t in range(PACK):
+            if t % 2 == 0:
+                nc.scalar.copy(out=prop_bf[:, t, :], in_=acc[t][:])
+            else:
+                nc.vector.tensor_copy(out=prop_bf[:, t, :], in_=acc[t][:])
+        prop_grouped = consts.tile([P, NODES, PACK], BF16, align_bytes=64)
+        nc.vector.tensor_copy(out=prop_grouped[:], in_=prop_bf[:].rearrange("p t n -> p n t"))
+        prop_codes = consts.tile([P, NODES], U32, align_bytes=64)
+        prop_scales = consts.tile([P, NODES], U8, align_bytes=64)
+        nc.vector.quantize_mx(
+            out=prop_codes[:].bitcast(FP8X4),
+            scales=prop_scales[:],
+            in_=prop_grouped[:].rearrange("p n t -> p (n t)"),
+        )
+        for a in range(NODE_TILES):
+            product = bank_pool.tile([P, CHANNELS], F32, name="product", tag="bank")
+            nc.tensor.matmul_mx(
+                out=product[:],
+                lhsT=prop_codes[:, a * P : (a + 1) * P].bitcast(FP8X4),
+                lhsT_scale=prop_scales[:, a * P : (a + 1) * P],
+                rhs=w2_codes[:].bitcast(FP8X4),
+                rhs_scale=w2_scales[:],
+                start=True,
+                stop=True,
+            )
+            result = out_pool.tile([P, CHANNELS], F32, name="result")
+            nc.vector.tensor_tensor(out=result[:], in0=product[:], in1=residual[:, a, :], op=ADD)
+            nc.sync.dma_start(out=out[a * P : (a + 1) * P, :], in_=result[:])

@@ -29,7 +29,7 @@ HE_BUFS = 6
 HE_COLS = PACK * CHANNELS
 INC_COLS = PACK * NODES
 BANK_WORDS = 512
-VECTOR_WORDS = 80
+VECTOR_WORDS = 96
 
 FLOPS = 2 * NODES * EDGES * CHANNELS + 2 * NODES * CHANNELS * CHANNELS
 

@@ -20,18 +20,27 @@ EDGES = 16384
 CHANNELS = 512
 NODE_TILES = NODES // P
 PASSES = EDGES // K_PASS
+PASS_WORDS = K_PASS // 2
+BANK_WORDS = 512
 
-CHUNK_PASSES = 4
-CHUNK_EDGES = CHUNK_PASSES * K_PASS
+MAX_CHUNK = 4
+MIN_CHUNK = 2
 INC_BUFS = 3
 HE_BUFS = 6
 
-HE_COLS = PACK * CHANNELS
-INC_COLS = PACK * NODES
-BANK_WORDS = 512
-VECTOR_WORDS = 96
+VECTOR_WORDS = 80
 
 FLOPS = 2 * NODES * EDGES * CHANNELS + 2 * NODES * CHANNELS * CHANNELS
+
+
+def incidence_chunks():
+    chunks = []
+    first = 0
+    while first < PASSES:
+        passes = max(MIN_CHUNK, min(MAX_CHUNK, (PASSES - first) // 2))
+        chunks.append((first, passes))
+        first += passes
+    return chunks
 
 
 def tile_heterogeneoustemporalhypergraphnn_pb_k_kernel(
@@ -42,18 +51,22 @@ def tile_heterogeneoustemporalhypergraphnn_pb_k_kernel(
         consts = ctx.enter_context(tc.tile_pool(name="consts", bufs=1))
         inc_pool = ctx.enter_context(tc.tile_pool(name="inc", bufs=INC_BUFS))
         he_pool = ctx.enter_context(tc.tile_pool(name="he", bufs=HE_BUFS))
-        grouped_pool = ctx.enter_context(tc.tile_pool(name="grouped", bufs=4))
-        mx_pool = ctx.enter_context(tc.tile_pool(name="mx", bufs=3))
+        grouped_pool = ctx.enter_context(tc.tile_pool(name="grouped", bufs=3))
+        mx_pool = ctx.enter_context(tc.tile_pool(name="mx", bufs=4))
         out_pool = ctx.enter_context(tc.tile_pool(name="out", bufs=NODE_TILES))
         acc_pool = ctx.enter_context(tc.psum_pool(name="acc", bufs=1))
         bank_pool = ctx.enter_context(tc.psum_pool(name="bank", bufs=4))
         ctx.enter_context(tc.manual_schedule())
 
+        incidence_by_tile = incidence.rearrange("(p a) k -> p a k", a=NODE_TILES)
+        features_by_tile = node_features.rearrange("(p a) c -> p a c", a=NODE_TILES)
+        out_by_tile = out.rearrange("(p a) c -> p a c", a=NODE_TILES)
+
         identity = consts.tile([P, P], F32)
         make_identity(nc, identity[:])
 
         features = consts.tile([P, NODE_TILES, CHANNELS], BF16)
-        nc.sync.dma_start(out=features[:], in_=node_features.rearrange("(a p) c -> p a c", p=P))
+        nc.sync.dma_start(out=features[:], in_=features_by_tile)
 
         w2_codes = consts.tile([P, CHANNELS], U32, align_bytes=64)
         nc.sync.dma_start(
@@ -83,18 +96,27 @@ def tile_heterogeneoustemporalhypergraphnn_pb_k_kernel(
 
         acc = [acc_pool.tile([P, NODES], F32, name="acc%d" % t) for t in range(PACK)]
 
-        incidence_by_tile = incidence.rearrange("(a p) k -> p a k", p=P)
+        chunk_passes = dict(incidence_chunks())
+        chunk_first = {}
+        for first, passes in chunk_passes.items():
+            for g in range(first, first + passes):
+                chunk_first[g] = first
+
         inc_raw = {}
         he_raw = {}
-        grouped = {}
-        codes = {}
-        scales = {}
+        inc_grouped = {}
+        he_grouped = {}
+        inc_codes = {}
+        inc_scales = {}
+        he_codes = {}
+        he_scales = {}
 
-        def load_incidence(chunk):
-            inc_raw[chunk] = inc_pool.tile([P, NODE_TILES, CHUNK_EDGES], BF16, name="inc_raw")
+        def load_incidence(first):
+            edges = chunk_passes[first] * K_PASS
+            inc_raw[first] = inc_pool.tile([P, NODE_TILES, edges], BF16, name="inc_raw")
             nc.sync.dma_start(
-                out=inc_raw[chunk][:],
-                in_=incidence_by_tile[:, :, chunk * CHUNK_EDGES : (chunk + 1) * CHUNK_EDGES],
+                out=inc_raw[first][:],
+                in_=incidence_by_tile[:, :, first * K_PASS : first * K_PASS + edges],
             )
 
         def load_he(g):
@@ -105,48 +127,60 @@ def tile_heterogeneoustemporalhypergraphnn_pb_k_kernel(
             )
 
         def load_for(g):
-            if (g + 1) % CHUNK_PASSES == 0 and g + 1 < PASSES:
-                load_incidence((g + 1) // CHUNK_PASSES)
+            if g + 1 in chunk_passes:
+                load_incidence(g + 1)
             load_he(g)
 
         def transpose_incidence(g):
-            grouped[g] = grouped_pool.tile([P, HE_COLS + INC_COLS], BF16, name="grouped", align_bytes=64)
-            words = inc_raw[g // CHUNK_PASSES][:].bitcast(F32)
-            first = (g % CHUNK_PASSES) * (K_PASS // 2)
-            inc_words = grouped[g][:, HE_COLS:].bitcast(F32)
+            inc_grouped[g] = grouped_pool.tile([P, PACK * NODES], BF16, name="inc_grouped", align_bytes=64)
+            words = inc_raw[chunk_first[g]][:].bitcast(F32)
+            first_word = (g - chunk_first[g]) * PASS_WORDS
+            grouped_words = inc_grouped[g][:].bitcast(F32)
             for half in range(2):
                 bank = bank_pool.tile([P, 2, 2 * P], F32, name="xt", tag="bank")
                 for a in range(2):
                     for u in range(2):
                         nc.tensor.transpose(
                             out=bank[:, u, a * P : (a + 1) * P],
-                            in_=words[:, 2 * half + a, first + u * P : first + (u + 1) * P],
+                            in_=words[:, 2 * half + a, first_word + u * P : first_word + (u + 1) * P],
                             identity=identity[:],
                         )
                 nc.scalar.copy(
-                    out=inc_words[:, half * BANK_WORDS : (half + 1) * BANK_WORDS].rearrange("p (n u) -> p n u", u=2),
+                    out=grouped_words[:, half * BANK_WORDS : (half + 1) * BANK_WORDS].rearrange(
+                        "p (n u) -> p n u", u=2
+                    ),
                     in_=bank[:].rearrange("p u n -> p n u"),
                 )
 
+        def quantise_incidence(g):
+            inc_codes[g] = mx_pool.tile([P, NODES], U32, name="inc_codes", align_bytes=64)
+            inc_scales[g] = mx_pool.tile([P, NODES], U8, name="inc_scales", align_bytes=64)
+            nc.vector.quantize_mx(
+                out=inc_codes[g][:].bitcast(FP8X4), scales=inc_scales[g][:], in_=inc_grouped[g][:]
+            )
+
         def regroup_he(g):
+            he_grouped[g] = grouped_pool.tile([P, PACK * CHANNELS], BF16, name="he_grouped", align_bytes=64)
             src = he_raw[g][:].rearrange("q j (p t) -> q p j t", t=PACK)
-            dst = grouped[g][:, 0:HE_COLS].rearrange("q (t p j) -> q p j t", t=PACK, j=PACK)
+            dst = he_grouped[g][:].rearrange("q (t p j) -> q p j t", t=PACK, j=PACK)
             nc.vector.tensor_copy(out=dst[:, 0:VECTOR_WORDS], in_=src[:, 0:VECTOR_WORDS])
             nc.scalar.copy(out=dst[:, VECTOR_WORDS:P], in_=src[:, VECTOR_WORDS:P])
 
-        def quantise(g):
-            codes[g] = mx_pool.tile([P, CHANNELS + NODES], U32, name="codes", align_bytes=64)
-            scales[g] = mx_pool.tile([P, CHANNELS + NODES], U8, name="scales", align_bytes=64)
-            nc.vector.quantize_mx(out=codes[g][:].bitcast(FP8X4), scales=scales[g][:], in_=grouped[g][:])
+        def quantise_he(g):
+            he_codes[g] = mx_pool.tile([P, CHANNELS], U32, name="he_codes", align_bytes=64)
+            he_scales[g] = mx_pool.tile([P, CHANNELS], U8, name="he_scales", align_bytes=64)
+            nc.vector.quantize_mx(
+                out=he_codes[g][:].bitcast(FP8X4), scales=he_scales[g][:], in_=he_grouped[g][:]
+            )
 
         def multiply(g):
             for t in range(PACK):
                 nc.tensor.matmul_mx(
                     out=acc[t][:],
-                    lhsT=codes[g][:, t * P : (t + 1) * P].bitcast(FP8X4),
-                    lhsT_scale=scales[g][:, t * P : (t + 1) * P],
-                    rhs=codes[g][:, CHANNELS:].bitcast(FP8X4),
-                    rhs_scale=scales[g][:, CHANNELS:],
+                    lhsT=he_codes[g][:, t * P : (t + 1) * P].bitcast(FP8X4),
+                    lhsT_scale=he_scales[g][:, t * P : (t + 1) * P],
+                    rhs=inc_codes[g][:].bitcast(FP8X4),
+                    rhs_scale=inc_scales[g][:],
                     start=(g == 0),
                     stop=(g == PASSES - 1),
                 )
@@ -159,9 +193,11 @@ def tile_heterogeneoustemporalhypergraphnn_pb_k_kernel(
             if 0 <= step + 1 < PASSES:
                 transpose_incidence(step + 1)
             if 0 <= step < PASSES:
-                regroup_he(step)
+                quantise_incidence(step)
             if 0 <= step - 1 < PASSES:
-                quantise(step - 1)
+                quantise_he(step - 1)
+            if 0 <= step < PASSES:
+                regroup_he(step)
             if 0 <= step - 2 < PASSES:
                 multiply(step - 2)
             if 0 <= step and step + HE_BUFS < PASSES:
@@ -173,15 +209,20 @@ def tile_heterogeneoustemporalhypergraphnn_pb_k_kernel(
                 nc.scalar.copy(out=prop_bf[:, t, :], in_=acc[t][:])
             else:
                 nc.vector.tensor_copy(out=prop_bf[:, t, :], in_=acc[t][:])
+        half_nodes = NODES // 2
         prop_grouped = consts.tile([P, NODES, PACK], BF16, align_bytes=64)
-        nc.vector.tensor_copy(out=prop_grouped[:], in_=prop_bf[:].rearrange("p t n -> p n t"))
+        prop_by_node = prop_bf[:].rearrange("p t n -> p n t")
+        nc.vector.tensor_copy(out=prop_grouped[:, 0:half_nodes, :], in_=prop_by_node[:, 0:half_nodes, :])
+        nc.scalar.copy(out=prop_grouped[:, half_nodes:NODES, :], in_=prop_by_node[:, half_nodes:NODES, :])
         prop_codes = consts.tile([P, NODES], U32, align_bytes=64)
         prop_scales = consts.tile([P, NODES], U8, align_bytes=64)
-        nc.vector.quantize_mx(
-            out=prop_codes[:].bitcast(FP8X4),
-            scales=prop_scales[:],
-            in_=prop_grouped[:].rearrange("p n t -> p (n t)"),
-        )
+        for half in range(2):
+            nodes = slice(half * half_nodes, (half + 1) * half_nodes)
+            nc.vector.quantize_mx(
+                out=prop_codes[:, nodes].bitcast(FP8X4),
+                scales=prop_scales[:, nodes],
+                in_=prop_grouped[:, nodes, :].rearrange("p n t -> p (n t)"),
+            )
         for a in range(NODE_TILES):
             product = bank_pool.tile([P, CHANNELS], F32, name="product", tag="bank")
             nc.tensor.matmul_mx(
@@ -195,4 +236,4 @@ def tile_heterogeneoustemporalhypergraphnn_pb_k_kernel(
             )
             result = out_pool.tile([P, CHANNELS], F32, name="result")
             nc.vector.tensor_tensor(out=result[:], in0=product[:], in1=residual[:, a, :], op=ADD)
-            nc.sync.dma_start(out=out[a * P : (a + 1) * P, :], in_=result[:])
+            nc.sync.dma_start(out=out_by_tile[:, a, :], in_=result[:])

@@ -25,6 +25,7 @@ BANK_WORDS = 512
 
 MAX_CHUNK = 4
 MIN_CHUNK = 2
+RUN_PASSES = 2
 INC_BUFS = 3
 HE_BUFS = 6
 
@@ -51,7 +52,8 @@ def tile_heterogeneoustemporalhypergraphnn_pb_k_kernel(
         consts = ctx.enter_context(tc.tile_pool(name="consts", bufs=1))
         inc_pool = ctx.enter_context(tc.tile_pool(name="inc", bufs=INC_BUFS))
         he_pool = ctx.enter_context(tc.tile_pool(name="he", bufs=HE_BUFS))
-        grouped_pool = ctx.enter_context(tc.tile_pool(name="grouped", bufs=3))
+        inc_grouped_pool = ctx.enter_context(tc.tile_pool(name="inc_grouped", bufs=2 * RUN_PASSES))
+        he_grouped_pool = ctx.enter_context(tc.tile_pool(name="he_grouped", bufs=3))
         mx_pool = ctx.enter_context(tc.tile_pool(name="mx", bufs=4))
         out_pool = ctx.enter_context(tc.tile_pool(name="out", bufs=NODE_TILES))
         acc_pool = ctx.enter_context(tc.psum_pool(name="acc", bufs=1))
@@ -127,12 +129,12 @@ def tile_heterogeneoustemporalhypergraphnn_pb_k_kernel(
             )
 
         def load_for(g):
-            if g + 1 in chunk_passes:
-                load_incidence(g + 1)
+            if g + RUN_PASSES in chunk_passes:
+                load_incidence(g + RUN_PASSES)
             load_he(g)
 
         def transpose_incidence(g):
-            inc_grouped[g] = grouped_pool.tile([P, PACK * NODES], BF16, name="inc_grouped", align_bytes=64)
+            inc_grouped[g] = inc_grouped_pool.tile([P, PACK * NODES], BF16, name="inc_grouped", align_bytes=64)
             words = inc_raw[chunk_first[g]][:].bitcast(F32)
             first_word = (g - chunk_first[g]) * PASS_WORDS
             grouped_words = inc_grouped[g][:].bitcast(F32)
@@ -160,7 +162,7 @@ def tile_heterogeneoustemporalhypergraphnn_pb_k_kernel(
             )
 
         def regroup_he(g):
-            he_grouped[g] = grouped_pool.tile([P, PACK * CHANNELS], BF16, name="he_grouped", align_bytes=64)
+            he_grouped[g] = he_grouped_pool.tile([P, PACK * CHANNELS], BF16, name="he_grouped", align_bytes=64)
             src = he_raw[g][:].rearrange("q j (p t) -> q p j t", t=PACK)
             dst = he_grouped[g][:].rearrange("q (t p j) -> q p j t", t=PACK, j=PACK)
             nc.vector.tensor_copy(out=dst[:, 0:VECTOR_WORDS], in_=src[:, 0:VECTOR_WORDS])
@@ -189,19 +191,22 @@ def tile_heterogeneoustemporalhypergraphnn_pb_k_kernel(
         for g in range(HE_BUFS):
             load_for(g)
 
-        for step in range(-1, PASSES + 2):
-            if 0 <= step + 1 < PASSES:
-                transpose_incidence(step + 1)
-            if 0 <= step < PASSES:
-                quantise_incidence(step)
-            if 0 <= step - 1 < PASSES:
-                quantise_he(step - 1)
-            if 0 <= step < PASSES:
-                regroup_he(step)
-            if 0 <= step - 2 < PASSES:
-                multiply(step - 2)
-            if 0 <= step and step + HE_BUFS < PASSES:
-                load_for(step + HE_BUFS)
+        for run_first in range(-RUN_PASSES, PASSES + RUN_PASSES, RUN_PASSES):
+            for g in range(run_first + RUN_PASSES, run_first + 2 * RUN_PASSES):
+                if g < PASSES:
+                    transpose_incidence(g)
+            for g in range(run_first, run_first + RUN_PASSES):
+                if 0 <= g < PASSES:
+                    quantise_incidence(g)
+                if 0 <= g - 1 < PASSES:
+                    quantise_he(g - 1)
+                if 0 <= g < PASSES:
+                    regroup_he(g)
+                if 0 <= g and g + HE_BUFS < PASSES:
+                    load_for(g + HE_BUFS)
+            for g in range(run_first - RUN_PASSES, run_first):
+                if 0 <= g:
+                    multiply(g)
 
         prop_bf = consts.tile([P, PACK, NODES], BF16)
         for t in range(PACK):

@@ -25,11 +25,10 @@ BANK_WORDS = 512
 
 MAX_CHUNK = 4
 MIN_CHUNK = 2
-RUN_PASSES = 2
 INC_BUFS = 3
 HE_BUFS = 6
 
-VECTOR_WORDS = 80
+VECTOR_WORDS = 88
 
 FLOPS = 2 * NODES * EDGES * CHANNELS + 2 * NODES * CHANNELS * CHANNELS
 
@@ -52,8 +51,7 @@ def tile_heterogeneoustemporalhypergraphnn_pb_k_kernel(
         consts = ctx.enter_context(tc.tile_pool(name="consts", bufs=1))
         inc_pool = ctx.enter_context(tc.tile_pool(name="inc", bufs=INC_BUFS))
         he_pool = ctx.enter_context(tc.tile_pool(name="he", bufs=HE_BUFS))
-        inc_grouped_pool = ctx.enter_context(tc.tile_pool(name="inc_grouped", bufs=2 * RUN_PASSES))
-        he_grouped_pool = ctx.enter_context(tc.tile_pool(name="he_grouped", bufs=3))
+        grouped_pool = ctx.enter_context(tc.tile_pool(name="grouped", bufs=3))
         mx_pool = ctx.enter_context(tc.tile_pool(name="mx", bufs=4))
         out_pool = ctx.enter_context(tc.tile_pool(name="out", bufs=NODE_TILES))
         acc_pool = ctx.enter_context(tc.psum_pool(name="acc", bufs=1))
@@ -70,12 +68,6 @@ def tile_heterogeneoustemporalhypergraphnn_pb_k_kernel(
         features = consts.tile([P, NODE_TILES, CHANNELS], BF16)
         nc.sync.dma_start(out=features[:], in_=features_by_tile)
 
-        w2_codes = consts.tile([P, CHANNELS], U32, align_bytes=64)
-        nc.sync.dma_start(
-            out=w2_codes[:].bitcast(I32),
-            in_=W2_words[0].rearrange("p n t -> p (n t)").bitcast(I32),
-        )
-
         ones = consts.tile([P, P], BF16)
         nc.vector.memset(ones[:], 1.0)
         bias_rows = consts.tile([P, CHANNELS], BF16)
@@ -84,11 +76,6 @@ def tile_heterogeneoustemporalhypergraphnn_pb_k_kernel(
 
         w2_scales = consts.tile([P, CHANNELS], U8, align_bytes=64)
         nc.vector.memset(w2_scales[:].bitcast(I32), 0)
-        for quadrant in range(4):
-            nc.sync.dma_start(
-                out=w2_scales[32 * quadrant : 32 * quadrant + 4, :].bitcast(I32),
-                in_=W2_scales[0, 4 * quadrant : 4 * quadrant + 4, :].bitcast(I32),
-            )
 
         bias_bank = bank_pool.tile([P, CHANNELS], F32, name="bias_bank", tag="bank")
         nc.tensor.matmul(out=bias_bank[:], lhsT=ones[:], rhs=bias_rows[:], start=True, stop=True)
@@ -129,12 +116,12 @@ def tile_heterogeneoustemporalhypergraphnn_pb_k_kernel(
             )
 
         def load_for(g):
-            if g + RUN_PASSES in chunk_passes:
-                load_incidence(g + RUN_PASSES)
+            if g + 1 in chunk_passes:
+                load_incidence(g + 1)
             load_he(g)
 
         def transpose_incidence(g):
-            inc_grouped[g] = inc_grouped_pool.tile([P, PACK * NODES], BF16, name="inc_grouped", align_bytes=64)
+            inc_grouped[g] = grouped_pool.tile([P, PACK * NODES], BF16, name="inc_grouped", align_bytes=64)
             words = inc_raw[chunk_first[g]][:].bitcast(F32)
             first_word = (g - chunk_first[g]) * PASS_WORDS
             grouped_words = inc_grouped[g][:].bitcast(F32)
@@ -162,7 +149,7 @@ def tile_heterogeneoustemporalhypergraphnn_pb_k_kernel(
             )
 
         def regroup_he(g):
-            he_grouped[g] = he_grouped_pool.tile([P, PACK * CHANNELS], BF16, name="he_grouped", align_bytes=64)
+            he_grouped[g] = grouped_pool.tile([P, PACK * CHANNELS], BF16, name="he_grouped", align_bytes=64)
             src = he_raw[g][:].rearrange("q j (p t) -> q p j t", t=PACK)
             dst = he_grouped[g][:].rearrange("q (t p j) -> q p j t", t=PACK, j=PACK)
             nc.vector.tensor_copy(out=dst[:, 0:VECTOR_WORDS], in_=src[:, 0:VECTOR_WORDS])
@@ -191,22 +178,30 @@ def tile_heterogeneoustemporalhypergraphnn_pb_k_kernel(
         for g in range(HE_BUFS):
             load_for(g)
 
-        for run_first in range(-RUN_PASSES, PASSES + RUN_PASSES, RUN_PASSES):
-            for g in range(run_first + RUN_PASSES, run_first + 2 * RUN_PASSES):
-                if g < PASSES:
-                    transpose_incidence(g)
-            for g in range(run_first, run_first + RUN_PASSES):
-                if 0 <= g < PASSES:
-                    quantise_incidence(g)
-                if 0 <= g - 1 < PASSES:
-                    quantise_he(g - 1)
-                if 0 <= g < PASSES:
-                    regroup_he(g)
-                if 0 <= g and g + HE_BUFS < PASSES:
-                    load_for(g + HE_BUFS)
-            for g in range(run_first - RUN_PASSES, run_first):
-                if 0 <= g:
-                    multiply(g)
+        for step in range(-1, PASSES + 2):
+            if 0 <= step + 1 < PASSES:
+                transpose_incidence(step + 1)
+            if 0 <= step < PASSES:
+                quantise_incidence(step)
+            if 0 <= step - 1 < PASSES:
+                quantise_he(step - 1)
+            if 0 <= step < PASSES:
+                regroup_he(step)
+            if 0 <= step - 2 < PASSES:
+                multiply(step - 2)
+            if 0 <= step and step + HE_BUFS < PASSES:
+                load_for(step + HE_BUFS)
+
+        w2_codes = consts.tile([P, CHANNELS], U32, align_bytes=64)
+        nc.sync.dma_start(
+            out=w2_codes[:].bitcast(I32),
+            in_=W2_words[0].rearrange("p n t -> p (n t)").bitcast(I32),
+        )
+        for quadrant in range(4):
+            nc.sync.dma_start(
+                out=w2_scales[32 * quadrant : 32 * quadrant + 4, :].bitcast(I32),
+                in_=W2_scales[0, 4 * quadrant : 4 * quadrant + 4, :].bitcast(I32),
+            )
 
         prop_bf = consts.tile([P, PACK, NODES], BF16)
         for t in range(PACK):

@@ -24,11 +24,14 @@ PASS_WORDS = K_PASS // 2
 BANK_WORDS = 512
 
 MAX_CHUNK = 4
-MIN_CHUNK = 2
 INC_BUFS = 3
 HE_BUFS = 6
 
-VECTOR_WORDS = 88
+GROUP = 4
+CHANNEL_GROUPS = CHANNELS // GROUP
+VECTOR_GROUPS = 88
+LAST = PASSES - 1
+W2_PASSES_AHEAD = 4
 
 FLOPS = 2 * NODES * EDGES * CHANNELS + 2 * NODES * CHANNELS * CHANNELS
 
@@ -37,7 +40,7 @@ def incidence_chunks():
     chunks = []
     first = 0
     while first < PASSES:
-        passes = max(MIN_CHUNK, min(MAX_CHUNK, (PASSES - first) // 2))
+        passes = max(1, min(MAX_CHUNK, (PASSES - first) // 2))
         chunks.append((first, passes))
         first += passes
     return chunks
@@ -53,7 +56,7 @@ def tile_heterogeneoustemporalhypergraphnn_pb_k_kernel(
         he_pool = ctx.enter_context(tc.tile_pool(name="he", bufs=HE_BUFS))
         grouped_pool = ctx.enter_context(tc.tile_pool(name="grouped", bufs=3))
         mx_pool = ctx.enter_context(tc.tile_pool(name="mx", bufs=4))
-        out_pool = ctx.enter_context(tc.tile_pool(name="out", bufs=NODE_TILES))
+        tail_pool = ctx.enter_context(tc.tile_pool(name="tail", bufs=NODE_TILES))
         acc_pool = ctx.enter_context(tc.psum_pool(name="acc", bufs=1))
         bank_pool = ctx.enter_context(tc.psum_pool(name="bank", bufs=4))
         ctx.enter_context(tc.manual_schedule())
@@ -74,6 +77,7 @@ def tile_heterogeneoustemporalhypergraphnn_pb_k_kernel(
         nc.vector.memset(bias_rows[:], 0.0)
         nc.sync.dma_start(out=bias_rows[0:1, :], in_=b2.unsqueeze(0))
 
+        w2_codes = consts.tile([P, CHANNELS], U32, align_bytes=64)
         w2_scales = consts.tile([P, CHANNELS], U8, align_bytes=64)
         nc.vector.memset(w2_scales[:].bitcast(I32), 0)
 
@@ -83,7 +87,7 @@ def tile_heterogeneoustemporalhypergraphnn_pb_k_kernel(
         for a in range(NODE_TILES):
             nc.vector.tensor_tensor(out=residual[:, a, :], in0=bias_bank[:], in1=features[:, a, :], op=ADD)
 
-        acc = [acc_pool.tile([P, NODES], F32, name="acc%d" % t) for t in range(PACK)]
+        acc = [acc_pool.tile([P, CHANNELS], F32, name="acc%d" % a) for a in range(NODE_TILES)]
 
         chunk_passes = dict(incidence_chunks())
         chunk_first = {}
@@ -103,10 +107,12 @@ def tile_heterogeneoustemporalhypergraphnn_pb_k_kernel(
         def load_incidence(first):
             edges = chunk_passes[first] * K_PASS
             inc_raw[first] = inc_pool.tile([P, NODE_TILES, edges], BF16, name="inc_raw")
-            nc.sync.dma_start(
-                out=inc_raw[first][:],
-                in_=incidence_by_tile[:, :, first * K_PASS : first * K_PASS + edges],
-            )
+            tiles = 1 if first == LAST else NODE_TILES
+            for a in range(0, NODE_TILES, tiles):
+                nc.sync.dma_start(
+                    out=inc_raw[first][:, a : a + tiles, :],
+                    in_=incidence_by_tile[:, a : a + tiles, first * K_PASS : first * K_PASS + edges],
+                )
 
         def load_he(g):
             he_raw[g] = he_pool.tile([P, PACK, CHANNELS], BF16, name="he_raw")
@@ -116,9 +122,24 @@ def tile_heterogeneoustemporalhypergraphnn_pb_k_kernel(
             )
 
         def load_for(g):
-            if g + 1 in chunk_passes:
+            if g + 1 in chunk_passes and g + 1 != LAST:
                 load_incidence(g + 1)
+            if g == LAST - W2_PASSES_AHEAD:
+                load_w2()
             load_he(g)
+            if g == LAST:
+                load_incidence(LAST)
+
+        def load_w2():
+            nc.sync.dma_start(
+                out=w2_codes[:].bitcast(I32),
+                in_=W2_words[0].rearrange("p n t -> p (n t)").bitcast(I32),
+            )
+            for quadrant in range(4):
+                nc.sync.dma_start(
+                    out=w2_scales[32 * quadrant : 32 * quadrant + 4, :].bitcast(I32),
+                    in_=W2_scales[0, 4 * quadrant : 4 * quadrant + 4, :].bitcast(I32),
+                )
 
         def transpose_incidence(g):
             inc_grouped[g] = grouped_pool.tile([P, PACK * NODES], BF16, name="inc_grouped", align_bytes=64)
@@ -150,10 +171,10 @@ def tile_heterogeneoustemporalhypergraphnn_pb_k_kernel(
 
         def regroup_he(g):
             he_grouped[g] = grouped_pool.tile([P, PACK * CHANNELS], BF16, name="he_grouped", align_bytes=64)
-            src = he_raw[g][:].rearrange("q j (p t) -> q p j t", t=PACK)
-            dst = he_grouped[g][:].rearrange("q (t p j) -> q p j t", t=PACK, j=PACK)
-            nc.vector.tensor_copy(out=dst[:, 0:VECTOR_WORDS], in_=src[:, 0:VECTOR_WORDS])
-            nc.scalar.copy(out=dst[:, VECTOR_WORDS:P], in_=src[:, VECTOR_WORDS:P])
+            src = he_raw[g][:].rearrange("q j (c i) -> q c j i", i=GROUP)
+            dst = he_grouped[g][:].rearrange("q (c i j) -> q c j i", i=GROUP, j=PACK)
+            nc.vector.tensor_copy(out=dst[:, 0:VECTOR_GROUPS], in_=src[:, 0:VECTOR_GROUPS])
+            nc.scalar.copy(out=dst[:, VECTOR_GROUPS:CHANNEL_GROUPS], in_=src[:, VECTOR_GROUPS:CHANNEL_GROUPS])
 
         def quantise_he(g):
             he_codes[g] = mx_pool.tile([P, CHANNELS], U32, name="he_codes", align_bytes=64)
@@ -163,77 +184,109 @@ def tile_heterogeneoustemporalhypergraphnn_pb_k_kernel(
             )
 
         def multiply(g):
-            for t in range(PACK):
+            for a in range(NODE_TILES):
                 nc.tensor.matmul_mx(
-                    out=acc[t][:],
-                    lhsT=he_codes[g][:, t * P : (t + 1) * P].bitcast(FP8X4),
-                    lhsT_scale=he_scales[g][:, t * P : (t + 1) * P],
-                    rhs=inc_codes[g][:].bitcast(FP8X4),
-                    rhs_scale=inc_scales[g][:],
+                    out=acc[a][:],
+                    lhsT=inc_codes[g][:, a * P : (a + 1) * P].bitcast(FP8X4),
+                    lhsT_scale=inc_scales[g][:, a * P : (a + 1) * P],
+                    rhs=he_codes[g][:].bitcast(FP8X4),
+                    rhs_scale=he_scales[g][:],
                     start=(g == 0),
-                    stop=(g == PASSES - 1),
+                    stop=False,
                 )
 
         load_incidence(0)
         for g in range(HE_BUFS):
             load_for(g)
 
-        for step in range(-1, PASSES + 2):
-            if 0 <= step + 1 < PASSES:
+        for step in range(-1, PASSES + 1):
+            if 0 <= step + 1 < LAST:
                 transpose_incidence(step + 1)
-            if 0 <= step < PASSES:
+            if 0 <= step < LAST:
                 quantise_incidence(step)
-            if 0 <= step - 1 < PASSES:
+            if 0 <= step - 1:
                 quantise_he(step - 1)
             if 0 <= step < PASSES:
                 regroup_he(step)
-            if 0 <= step - 2 < PASSES:
+            if 0 <= step - 2:
                 multiply(step - 2)
             if 0 <= step and step + HE_BUFS < PASSES:
                 load_for(step + HE_BUFS)
 
-        w2_codes = consts.tile([P, CHANNELS], U32, align_bytes=64)
-        nc.sync.dma_start(
-            out=w2_codes[:].bitcast(I32),
-            in_=W2_words[0].rearrange("p n t -> p (n t)").bitcast(I32),
-        )
-        for quadrant in range(4):
-            nc.sync.dma_start(
-                out=w2_scales[32 * quadrant : 32 * quadrant + 4, :].bitcast(I32),
-                in_=W2_scales[0, 4 * quadrant : 4 * quadrant + 4, :].bitcast(I32),
-            )
+        last_bank = {}
+        last_codes = {}
+        last_scales = {}
+        prop_bf = {}
+        prop_bank = {}
+        prop_codes = {}
+        prop_scales = {}
 
-        prop_bf = consts.tile([P, PACK, NODES], BF16)
-        for t in range(PACK):
-            if t % 2 == 0:
-                nc.scalar.copy(out=prop_bf[:, t, :], in_=acc[t][:])
-            else:
-                nc.vector.tensor_copy(out=prop_bf[:, t, :], in_=acc[t][:])
-        half_nodes = NODES // 2
-        prop_grouped = consts.tile([P, NODES, PACK], BF16, align_bytes=64)
-        prop_by_node = prop_bf[:].rearrange("p t n -> p n t")
-        nc.vector.tensor_copy(out=prop_grouped[:, 0:half_nodes, :], in_=prop_by_node[:, 0:half_nodes, :])
-        nc.scalar.copy(out=prop_grouped[:, half_nodes:NODES, :], in_=prop_by_node[:, half_nodes:NODES, :])
-        prop_codes = consts.tile([P, NODES], U32, align_bytes=64)
-        prop_scales = consts.tile([P, NODES], U8, align_bytes=64)
-        for half in range(2):
-            nodes = slice(half * half_nodes, (half + 1) * half_nodes)
-            nc.vector.quantize_mx(
-                out=prop_codes[:, nodes].bitcast(FP8X4),
-                scales=prop_scales[:, nodes],
-                in_=prop_grouped[:, nodes, :].rearrange("p n t -> p (n t)"),
+        def regroup_words(bank, name):
+            grouped = tail_pool.tile([P, PACK * P], BF16, name=name, align_bytes=64)
+            nc.scalar.copy(
+                out=grouped[:].bitcast(F32).rearrange("p (n u) -> p n u", u=2),
+                in_=bank[:].rearrange("p u n -> p n u"),
             )
-        for a in range(NODE_TILES):
-            product = bank_pool.tile([P, CHANNELS], F32, name="product", tag="bank")
+            return grouped
+
+        def quantise_tile(grouped, name):
+            codes = tail_pool.tile([P, P], U32, name=name + "_codes", align_bytes=64)
+            scales = tail_pool.tile([P, P], U8, name=name + "_scales", align_bytes=64)
+            nc.vector.quantize_mx(out=codes[:].bitcast(FP8X4), scales=scales[:], in_=grouped[:])
+            return codes, scales
+
+        def transpose_words(words, name):
+            bank = bank_pool.tile([P, 2, P], F32, name=name, tag="bank")
+            for u in range(2):
+                nc.tensor.transpose(
+                    out=bank[:, u, :], in_=words[:, u * P : (u + 1) * P], identity=identity[:]
+                )
+            return bank
+
+        def finish_sums(a):
+            nc.tensor.matmul_mx(
+                out=acc[a][:],
+                lhsT=last_codes[a][:].bitcast(FP8X4),
+                lhsT_scale=last_scales[a][:],
+                rhs=he_codes[LAST][:].bitcast(FP8X4),
+                rhs_scale=he_scales[LAST][:],
+                start=False,
+                stop=True,
+            )
+            prop_bf[a] = tail_pool.tile([P, CHANNELS], BF16, name="prop_bf")
+            dst = prop_bf[a][:].rearrange("p (u w e) -> p u w e", u=2, e=2)
+            src = acc[a][:].rearrange("p (w u e) -> p u w e", u=2, e=2)
+            if a % 2 == 0:
+                nc.scalar.copy(out=dst, in_=src)
+            else:
+                nc.vector.tensor_copy(out=dst, in_=src)
+
+        def second_product(a):
+            product = acc_pool.tile([P, CHANNELS], F32, name="acc%d" % a)
             nc.tensor.matmul_mx(
                 out=product[:],
-                lhsT=prop_codes[:, a * P : (a + 1) * P].bitcast(FP8X4),
-                lhsT_scale=prop_scales[:, a * P : (a + 1) * P],
+                lhsT=prop_codes[a][:].bitcast(FP8X4),
+                lhsT_scale=prop_scales[a][:],
                 rhs=w2_codes[:].bitcast(FP8X4),
                 rhs_scale=w2_scales[:],
                 start=True,
                 stop=True,
             )
-            result = out_pool.tile([P, CHANNELS], F32, name="result")
+            result = tail_pool.tile([P, CHANNELS], F32, name="result")
             nc.vector.tensor_tensor(out=result[:], in0=product[:], in1=residual[:, a, :], op=ADD)
             nc.sync.dma_start(out=out_by_tile[:, a, :], in_=result[:])
+
+        for a in range(NODE_TILES):
+            last_bank[a] = transpose_words(inc_raw[LAST][:, a, :].bitcast(F32), "xt_last")
+        for a in range(NODE_TILES):
+            grouped = regroup_words(last_bank[a], "last_grouped")
+            last_codes[a], last_scales[a] = quantise_tile(grouped, "last")
+        for a in range(NODE_TILES):
+            finish_sums(a)
+        for a in range(NODE_TILES + 1):
+            if a < NODE_TILES:
+                prop_bank[a] = transpose_words(prop_bf[a][:].bitcast(F32), "pt")
+                grouped = regroup_words(prop_bank[a], "prop_grouped")
+                prop_codes[a], prop_scales[a] = quantise_tile(grouped, "prop")
+            if a > 0:
+                second_product(a - 1)

@@ -23,25 +23,37 @@ PASSES = EDGES // K_PASS
 PASS_WORDS = K_PASS // 2
 BANK_WORDS = 512
 
-MAX_CHUNK = 4
-INC_BUFS = 3
+MAX_CHUNK = 8
+INC_BUFS = 14
 HE_BUFS = 6
 
 GROUP = 4
 CHANNEL_GROUPS = CHANNELS // GROUP
 VECTOR_GROUPS = 88
 LAST = PASSES - 1
-W2_PASSES_AHEAD = 4
+W2_AT = 30
+SMALL_AT = 26
+RESIDUAL_AT = 29
+INC_AHEAD = 1
+LAST_BEFORE = 1
+ENDSEQ = "TsEviqM"
+HELD = 0
+MLAG = 3
+END_PASSES = 2
+VECTOR_GROUPS_END = 64
+VEVAC = (1, 3)
+VE2 = ()
 
 FLOPS = 2 * NODES * EDGES * CHANNELS + 2 * NODES * CHANNELS * CHANNELS
 
 
-def incidence_chunks():
+def incidence_chunks(a):
     chunks = []
     first = 0
     while first < PASSES:
-        passes = max(1, min(MAX_CHUNK, (PASSES - first) // 2))
-        chunks.append((first, passes))
+        longest = first + 3 if first else a + 1
+        passes = max(1, min(MAX_CHUNK, longest, (PASSES - first) // 2))
+        chunks.append(passes)
         first += passes
     return chunks
 
@@ -69,31 +81,39 @@ def tile_heterogeneoustemporalhypergraphnn_pb_k_kernel(
         make_identity(nc, identity[:])
 
         features = consts.tile([P, NODE_TILES, CHANNELS], BF16)
-        nc.sync.dma_start(out=features[:], in_=features_by_tile)
 
         ones = consts.tile([P, P], BF16)
         nc.vector.memset(ones[:], 1.0)
         bias_rows = consts.tile([P, CHANNELS], BF16)
         nc.vector.memset(bias_rows[:], 0.0)
-        nc.sync.dma_start(out=bias_rows[0:1, :], in_=b2.unsqueeze(0))
 
         w2_codes = consts.tile([P, CHANNELS], U32, align_bytes=64)
         w2_scales = consts.tile([P, CHANNELS], U8, align_bytes=64)
         nc.vector.memset(w2_scales[:].bitcast(I32), 0)
 
-        bias_bank = bank_pool.tile([P, CHANNELS], F32, name="bias_bank", tag="bank")
-        nc.tensor.matmul(out=bias_bank[:], lhsT=ones[:], rhs=bias_rows[:], start=True, stop=True)
+        bias = consts.tile([P, CHANNELS], F32)
+
+        def spread_bias():
+            bias_bank = bank_pool.tile([P, CHANNELS], F32, name="bias_bank", tag="bank")
+            nc.tensor.matmul(out=bias_bank[:], lhsT=ones[:], rhs=bias_rows[:], start=True, stop=True)
+            nc.vector.tensor_copy(out=bias[:], in_=bias_bank[:])
+
         residual = consts.tile([P, NODE_TILES, CHANNELS], F32)
-        for a in range(NODE_TILES):
-            nc.vector.tensor_tensor(out=residual[:, a, :], in0=bias_bank[:], in1=features[:, a, :], op=ADD)
+
+        def add_residual(a):
+            nc.vector.tensor_tensor(out=residual[:, a, :], in0=bias[:], in1=features[:, a, :], op=ADD)
 
         acc = [acc_pool.tile([P, CHANNELS], F32, name="acc%d" % a) for a in range(NODE_TILES)]
 
-        chunk_passes = dict(incidence_chunks())
+        chunk_passes = {}
         chunk_first = {}
-        for first, passes in chunk_passes.items():
-            for g in range(first, first + passes):
-                chunk_first[g] = first
+        for a in range(NODE_TILES):
+            first = 0
+            for passes in incidence_chunks(a):
+                chunk_passes[first, a] = passes
+                for g in range(first, first + passes):
+                    chunk_first[g, a] = first
+                first += passes
 
         inc_raw = {}
         he_raw = {}
@@ -105,14 +125,14 @@ def tile_heterogeneoustemporalhypergraphnn_pb_k_kernel(
         he_scales = {}
 
         def load_incidence(first):
-            edges = chunk_passes[first] * K_PASS
-            inc_raw[first] = inc_pool.tile([P, NODE_TILES, edges], BF16, name="inc_raw")
-            tiles = 1 if first == LAST else NODE_TILES
-            for a in range(0, NODE_TILES, tiles):
-                nc.sync.dma_start(
-                    out=inc_raw[first][:, a : a + tiles, :],
-                    in_=incidence_by_tile[:, a : a + tiles, first * K_PASS : first * K_PASS + edges],
-                )
+            for a in range(NODE_TILES):
+                if (first, a) in chunk_passes:
+                    edges = chunk_passes[first, a] * K_PASS
+                    inc_raw[first, a] = inc_pool.tile([P, edges], BF16, name="inc_raw")
+                    nc.sync.dma_start(
+                        out=inc_raw[first, a][:],
+                        in_=incidence_by_tile[:, a, first * K_PASS : first * K_PASS + edges],
+                    )
 
         def load_he(g):
             he_raw[g] = he_pool.tile([P, PACK, CHANNELS], BF16, name="he_raw")
@@ -122,12 +142,16 @@ def tile_heterogeneoustemporalhypergraphnn_pb_k_kernel(
             )
 
         def load_for(g):
-            if g + 1 in chunk_passes and g + 1 != LAST:
-                load_incidence(g + 1)
-            if g == LAST - W2_PASSES_AHEAD:
+            if g + INC_AHEAD < LAST and g + INC_AHEAD > 0:
+                load_incidence(g + INC_AHEAD)
+            if g == W2_AT:
                 load_w2()
-            load_he(g)
-            if g == LAST:
+            if g == SMALL_AT:
+                nc.sync.dma_start(out=bias_rows[0:1, :], in_=b2.unsqueeze(0))
+                nc.sync.dma_start(out=features[:], in_=features_by_tile)
+            if g >= 0:
+                load_he(g)
+            if g == LAST - LAST_BEFORE:
                 load_incidence(LAST)
 
         def load_w2():
@@ -141,20 +165,29 @@ def tile_heterogeneoustemporalhypergraphnn_pb_k_kernel(
                     in_=W2_scales[0, 4 * quadrant : 4 * quadrant + 4, :].bitcast(I32),
                 )
 
+        xb = {}
+
         def transpose_incidence(g):
             inc_grouped[g] = grouped_pool.tile([P, PACK * NODES], BF16, name="inc_grouped", align_bytes=64)
-            words = inc_raw[chunk_first[g]][:].bitcast(F32)
-            first_word = (g - chunk_first[g]) * PASS_WORDS
             grouped_words = inc_grouped[g][:].bitcast(F32)
             for half in range(2):
                 bank = bank_pool.tile([P, 2, 2 * P], F32, name="xt", tag="bank")
-                for a in range(2):
+                for i in range(2):
+                    a = 2 * half + i
+                    words = inc_raw[chunk_first[g, a], a][:].bitcast(F32)
+                    first_word = (g - chunk_first[g, a]) * PASS_WORDS
                     for u in range(2):
                         nc.tensor.transpose(
-                            out=bank[:, u, a * P : (a + 1) * P],
-                            in_=words[:, 2 * half + a, first_word + u * P : first_word + (u + 1) * P],
+                            out=bank[:, u, i * P : (i + 1) * P],
+                            in_=words[:, first_word + u * P : first_word + (u + 1) * P],
                             identity=identity[:],
                         )
+                xb[g, half] = bank
+
+        def evac(g):
+            grouped_words = inc_grouped[g][:].bitcast(F32)
+            for half in range(2):
+                bank = xb[g, half]
                 nc.scalar.copy(
                     out=grouped_words[:, half * BANK_WORDS : (half + 1) * BANK_WORDS].rearrange(
                         "p (n u) -> p n u", u=2
@@ -169,12 +202,25 @@ def tile_heterogeneoustemporalhypergraphnn_pb_k_kernel(
                 out=inc_codes[g][:].bitcast(FP8X4), scales=inc_scales[g][:], in_=inc_grouped[g][:]
             )
 
+        rr = {}
+
         def regroup_he(g):
+            if g in rr:
+                return
             he_grouped[g] = grouped_pool.tile([P, PACK * CHANNELS], BF16, name="he_grouped", align_bytes=64)
             src = he_raw[g][:].rearrange("q j (c i) -> q c j i", i=GROUP)
             dst = he_grouped[g][:].rearrange("q (c i j) -> q c j i", i=GROUP, j=PACK)
-            nc.vector.tensor_copy(out=dst[:, 0:VECTOR_GROUPS], in_=src[:, 0:VECTOR_GROUPS])
-            nc.scalar.copy(out=dst[:, VECTOR_GROUPS:CHANNEL_GROUPS], in_=src[:, VECTOR_GROUPS:CHANNEL_GROUPS])
+            rr[g] = (dst, src, VECTOR_GROUPS if g < PASSES - END_PASSES else VECTOR_GROUPS_END)
+
+        def rv(g):
+            regroup_he(g)
+            dst, src, split = rr[g]
+            nc.vector.tensor_copy(out=dst[:, 0:split], in_=src[:, 0:split])
+
+        def rs(g):
+            regroup_he(g)
+            dst, src, split = rr[g]
+            nc.scalar.copy(out=dst[:, split:CHANNEL_GROUPS], in_=src[:, split:CHANNEL_GROUPS])
 
         def quantise_he(g):
             he_codes[g] = mx_pool.tile([P, CHANNELS], U32, name="he_codes", align_bytes=64)
@@ -183,50 +229,43 @@ def tile_heterogeneoustemporalhypergraphnn_pb_k_kernel(
                 out=he_codes[g][:].bitcast(FP8X4), scales=he_scales[g][:], in_=he_grouped[g][:]
             )
 
-        def multiply(g):
-            for a in range(NODE_TILES):
-                nc.tensor.matmul_mx(
-                    out=acc[a][:],
-                    lhsT=inc_codes[g][:, a * P : (a + 1) * P].bitcast(FP8X4),
-                    lhsT_scale=inc_scales[g][:, a * P : (a + 1) * P],
-                    rhs=he_codes[g][:].bitcast(FP8X4),
-                    rhs_scale=he_scales[g][:],
-                    start=(g == 0),
-                    stop=False,
-                )
-
-        load_incidence(0)
-        for g in range(HE_BUFS):
-            load_for(g)
-
-        for step in range(-1, PASSES + 1):
-            if 0 <= step + 1 < LAST:
-                transpose_incidence(step + 1)
-            if 0 <= step < LAST:
-                quantise_incidence(step)
-            if 0 <= step - 1:
-                quantise_he(step - 1)
-            if 0 <= step < PASSES:
-                regroup_he(step)
-            if 0 <= step - 2:
-                multiply(step - 2)
-            if 0 <= step and step + HE_BUFS < PASSES:
-                load_for(step + HE_BUFS)
-
         last_bank = {}
+        last_grouped = {}
         last_codes = {}
         last_scales = {}
+
+        def multiply_tile(g, a):
+            if g == LAST:
+                codes, scales = last_codes[a][:], last_scales[a][:]
+            else:
+                nodes = slice(a * P, (a + 1) * P)
+                codes, scales = inc_codes[g][:, nodes], inc_scales[g][:, nodes]
+            nc.tensor.matmul_mx(
+                out=acc[a][:],
+                lhsT=codes.bitcast(FP8X4),
+                lhsT_scale=scales,
+                rhs=he_codes[g][:].bitcast(FP8X4),
+                rhs_scale=he_scales[g][:],
+                start=(g == 0),
+                stop=(g == LAST),
+            )
+
+        def multiply(g):
+            for a in range(NODE_TILES):
+                multiply_tile(g, a)
+
         prop_bf = {}
         prop_bank = {}
         prop_codes = {}
         prop_scales = {}
 
-        def regroup_words(bank, name):
+        def regroup_words(bank, name, vec=False):
             grouped = tail_pool.tile([P, PACK * P], BF16, name=name, align_bytes=64)
-            nc.scalar.copy(
-                out=grouped[:].bitcast(F32).rearrange("p (n u) -> p n u", u=2),
-                in_=bank[:].rearrange("p u n -> p n u"),
-            )
+            dst = grouped[:].bitcast(F32).rearrange("p (n u) -> p n u", u=2)
+            if vec:
+                nc.vector.tensor_copy(out=dst, in_=bank[:].rearrange("p u n -> p n u"))
+            else:
+                nc.scalar.copy(out=dst, in_=bank[:].rearrange("p u n -> p n u"))
             return grouped
 
         def quantise_tile(grouped, name):
@@ -244,19 +283,10 @@ def tile_heterogeneoustemporalhypergraphnn_pb_k_kernel(
             return bank
 
         def finish_sums(a):
-            nc.tensor.matmul_mx(
-                out=acc[a][:],
-                lhsT=last_codes[a][:].bitcast(FP8X4),
-                lhsT_scale=last_scales[a][:],
-                rhs=he_codes[LAST][:].bitcast(FP8X4),
-                rhs_scale=he_scales[LAST][:],
-                start=False,
-                stop=True,
-            )
             prop_bf[a] = tail_pool.tile([P, CHANNELS], BF16, name="prop_bf")
             dst = prop_bf[a][:].rearrange("p (u w e) -> p u w e", u=2, e=2)
             src = acc[a][:].rearrange("p (w u e) -> p u w e", u=2, e=2)
-            if a % 2 == 0:
+            if a not in VEVAC:
                 nc.scalar.copy(out=dst, in_=src)
             else:
                 nc.vector.tensor_copy(out=dst, in_=src)
@@ -276,17 +306,57 @@ def tile_heterogeneoustemporalhypergraphnn_pb_k_kernel(
             nc.vector.tensor_tensor(out=result[:], in0=product[:], in1=residual[:, a, :], op=ADD)
             nc.sync.dma_start(out=out_by_tile[:, a, :], in_=result[:])
 
-        for a in range(NODE_TILES):
-            last_bank[a] = transpose_words(inc_raw[LAST][:, a, :].bitcast(F32), "xt_last")
-        for a in range(NODE_TILES):
-            grouped = regroup_words(last_bank[a], "last_grouped")
-            last_codes[a], last_scales[a] = quantise_tile(grouped, "last")
-        for a in range(NODE_TILES):
-            finish_sums(a)
-        for a in range(NODE_TILES + 1):
+        A, B, CC, DD, SEQ = 1, 0, 0, 1, "TsEviqM"
+
+        def T(g):
+            if g < LAST:
+                transpose_incidence(g)
+            else:
+                for a in range(NODE_TILES):
+                    last_bank[a] = transpose_words(inc_raw[LAST, a][:].bitcast(F32), "xt_last")
+
+        def E(g):
+            if g < LAST:
+                evac(g)
+            else:
+                for a in range(NODE_TILES):
+                    last_grouped[a] = regroup_words(last_bank[a], "last_grouped")
+
+        def Q(g):
+            if g < LAST:
+                quantise_incidence(g)
+            else:
+                for a in range(NODE_TILES):
+                    last_codes[a], last_scales[a] = quantise_tile(last_grouped[a], "last")
+
+        def M(g):
+            if g < LAST - HELD:
+                multiply(g)
+            if g == LAST:
+                for a in range(NODE_TILES):
+                    for h in range(LAST - HELD, PASSES):
+                        multiply_tile(h, a)
+                    finish_sums(a)
+
+        load_incidence(0)
+        for g in range(-1, HE_BUFS):
+            load_for(g)
+        for step in range(-A, PASSES + DD):
+            for op in SEQ if step < PASSES - 2 else ENDSEQ:
+                f, g = {"T": (T, step + A), "E": (E, step + A), "i": (Q, step + B), "q": (quantise_he, step - CC), "v": (rv, step), "s": (rs, step), "M": (M, step - DD)}[op]
+                if 0 <= g < PASSES:
+                    f(g)
+            if step == RESIDUAL_AT - 1:
+                spread_bias()
+            if 0 <= step - RESIDUAL_AT < NODE_TILES:
+                add_residual(step - RESIDUAL_AT)
+            if 0 <= step and step + HE_BUFS < PASSES:
+                load_for(step + HE_BUFS)
+
+        for a in range(NODE_TILES + MLAG):
             if a < NODE_TILES:
                 prop_bank[a] = transpose_words(prop_bf[a][:].bitcast(F32), "pt")
-                grouped = regroup_words(prop_bank[a], "prop_grouped")
+                grouped = regroup_words(prop_bank[a], "prop_grouped", a in VE2)
                 prop_codes[a], prop_scales[a] = quantise_tile(grouped, "prop")
-            if a > 0:
-                second_product(a - 1)
+            if a >= MLAG:
+                second_product(a - MLAG)

@@ -32,15 +32,16 @@ CHANNEL_GROUPS = CHANNELS // GROUP
 VECTOR_GROUPS = 88
 LAST = PASSES - 1
 W2_AT = 30
-SMALL_AT = 26
-RESIDUAL_AT = 29
+SMALL_AT = 0
+RESIDUAL_AT = 2
+RES = {2: (0,), 3: (1,), 4: (2,), 5: (3,)}
 INC_AHEAD = 1
-LAST_BEFORE = 1
-ENDSEQ = "TsEviqM"
+LAST_BEFORE = 0
 HELD = 0
 MLAG = 3
-END_PASSES = 2
-VECTOR_GROUPS_END = 64
+SPLIT30 = 72
+SPLIT31 = 72
+TLAST = 1
 VEVAC = (1, 3)
 VE2 = ()
 
@@ -210,7 +211,7 @@ def tile_heterogeneoustemporalhypergraphnn_pb_k_kernel(
             he_grouped[g] = grouped_pool.tile([P, PACK * CHANNELS], BF16, name="he_grouped", align_bytes=64)
             src = he_raw[g][:].rearrange("q j (c i) -> q c j i", i=GROUP)
             dst = he_grouped[g][:].rearrange("q (c i j) -> q c j i", i=GROUP, j=PACK)
-            rr[g] = (dst, src, VECTOR_GROUPS if g < PASSES - END_PASSES else VECTOR_GROUPS_END)
+            rr[g] = (dst, src, {LAST - 1: SPLIT30, LAST: SPLIT31}.get(g, VECTOR_GROUPS))
 
         def rv(g):
             regroup_he(g)
@@ -342,14 +343,22 @@ def tile_heterogeneoustemporalhypergraphnn_pb_k_kernel(
         for g in range(-1, HE_BUFS):
             load_for(g)
         for step in range(-A, PASSES + DD):
-            for op in SEQ if step < PASSES - 2 else ENDSEQ:
+            for op in SEQ:
                 f, g = {"T": (T, step + A), "E": (E, step + A), "i": (Q, step + B), "q": (quantise_he, step - CC), "v": (rv, step), "s": (rs, step), "M": (M, step - DD)}[op]
-                if 0 <= g < PASSES:
+                if 0 <= g < (LAST if op in "TEi" else PASSES):
                     f(g)
+                if op == "s" and step == LAST and TLAST:
+                    T(LAST)
+                    E(LAST)
+            if step == LAST:
+                if not TLAST:
+                    T(LAST)
+                    E(LAST)
+                Q(LAST)
             if step == RESIDUAL_AT - 1:
                 spread_bias()
-            if 0 <= step - RESIDUAL_AT < NODE_TILES:
-                add_residual(step - RESIDUAL_AT)
+            for a in RES.get(step, ()):
+                add_residual(a)
             if 0 <= step and step + HE_BUFS < PASSES:
                 load_for(step + HE_BUFS)
 

@@ -31,7 +31,7 @@ GROUP = 4
 CHANNEL_GROUPS = CHANNELS // GROUP
 VECTOR_GROUPS = 88
 LAST = PASSES - 1
-W2_AT = 30
+W2_AT = 32
 SMALL_AT = 0
 RESIDUAL_AT = 2
 RES = {2: (0,), 3: (1,), 4: (2,), 5: (3,)}
@@ -154,6 +154,8 @@ def tile_heterogeneoustemporalhypergraphnn_pb_k_kernel(
                 load_he(g)
             if g == LAST - LAST_BEFORE:
                 load_incidence(LAST)
+            if g == LAST and W2_AT > LAST:
+                load_w2()
 
         def load_w2():
             nc.sync.dma_start(

@@ -23,7 +23,7 @@ PASSES = EDGES // K_PASS
 PASS_WORDS = K_PASS // 2
 BANK_WORDS = 512
 
-MAX_CHUNK = 8
+MAX_CHUNK = 6
 INC_BUFS = 14
 HE_BUFS = 6
 
@@ -32,6 +32,7 @@ CHANNEL_GROUPS = CHANNELS // GROUP
 VECTOR_GROUPS = 88
 LAST = PASSES - 1
 W2_AT = 32
+LONG_ROW_PASSES = 8
 SMALL_AT = 0
 RESIDUAL_AT = 2
 RES = {2: (0,), 3: (1,), 4: (2,), 5: (3,)}
@@ -137,10 +138,17 @@ def tile_heterogeneoustemporalhypergraphnn_pb_k_kernel(
 
         def load_he(g):
             he_raw[g] = he_pool.tile([P, PACK, CHANNELS], BF16, name="he_raw")
-            nc.sync.dma_start(
-                out=he_raw[g][:].rearrange("p (u e) c -> p u (e c)", u=2),
-                in_=he[g * K_PASS : (g + 1) * K_PASS, :].rearrange("(u p e) c -> p u (e c)", u=2, p=P),
-            )
+            rows = he[g * K_PASS : (g + 1) * K_PASS, :]
+            if g < LONG_ROW_PASSES:
+                nc.sync.dma_start(
+                    out=he_raw[g][:].rearrange("p t c -> p (t c)"),
+                    in_=rows.rearrange("(p t) c -> p (t c)", t=PACK),
+                )
+            else:
+                nc.sync.dma_start(
+                    out=he_raw[g][:].rearrange("p (u e) c -> p u (e c)", u=2),
+                    in_=rows.rearrange("(u p e) c -> p u (e c)", u=2, p=P),
+                )
 
         def load_for(g):
             if g + INC_AHEAD < LAST and g + INC_AHEAD > 0:
@@ -182,7 +190,11 @@ def tile_heterogeneoustemporalhypergraphnn_pb_k_kernel(
                     for u in range(2):
                         nc.tensor.transpose(
                             out=bank[:, u, i * P : (i + 1) * P],
-                            in_=words[:, first_word + u * P : first_word + (u + 1) * P],
+                            in_=(
+                                words[:, first_word + u : first_word + PASS_WORDS : 2]
+                                if g < LONG_ROW_PASSES
+                                else words[:, first_word + u * P : first_word + (u + 1) * P]
+                            ),
                             identity=identity[:],
                         )
                 xb[g, half] = bank

from contextlib import ExitStack

import concourse.mybir as mybir
from concourse.masks import make_identity

F32 = mybir.dt.float32
BF16 = mybir.dt.bfloat16
I32 = mybir.dt.int32
U32 = mybir.dt.uint32
U8 = mybir.dt.uint8
FP8X4 = mybir.dt.float8_e4m3fn_x4
ADD = mybir.AluOpType.add

P = 128
PACK = 4
K_PASS = P * PACK

NODES = 512
EDGES = 16384
CHANNELS = 512
NODE_TILES = NODES // P
PASSES = EDGES // K_PASS
PASS_WORDS = K_PASS // 2
BANK_WORDS = 512

MAX_CHUNK = 6
INC_BUFS = 14
HE_BUFS = 6

GROUP = 4
CHANNEL_GROUPS = CHANNELS // GROUP
VECTOR_GROUPS = 88
LAST = PASSES - 1
W2_AT = 32
LONG_ROW_PASSES = 8
SMALL_AT = 0
RESIDUAL_AT = 2
RES = {2: (0,), 3: (1,), 4: (2,), 5: (3,)}
INC_AHEAD = 1
LAST_BEFORE = 0
HELD = 0
MLAG = 3
SPLIT30 = 72
SPLIT31 = 72
TLAST = 1
VEVAC = (1, 3)
VE2 = ()

FLOPS = 2 * NODES * EDGES * CHANNELS + 2 * NODES * CHANNELS * CHANNELS


def incidence_chunks(a):
    chunks = []
    first = 0
    while first < PASSES:
        longest = first + 3 if first else a + 1
        passes = max(1, min(MAX_CHUNK, longest, (PASSES - first) // 2))
        chunks.append(passes)
        first += passes
    return chunks


def tile_heterogeneoustemporalhypergraphnn_pb_k_kernel(
    tc, incidence, he, W2_words, W2_scales, b2, node_features, out
):
    nc = tc.nc
    with ExitStack() as ctx:
        consts = ctx.enter_context(tc.tile_pool(name="consts", bufs=1))
        inc_pool = ctx.enter_context(tc.tile_pool(name="inc", bufs=INC_BUFS))
        he_pool = ctx.enter_context(tc.tile_pool(name="he", bufs=HE_BUFS))
        grouped_pool = ctx.enter_context(tc.tile_pool(name="grouped", bufs=3))
        mx_pool = ctx.enter_context(tc.tile_pool(name="mx", bufs=4))
        tail_pool = ctx.enter_context(tc.tile_pool(name="tail", bufs=NODE_TILES))
        acc_pool = ctx.enter_context(tc.psum_pool(name="acc", bufs=1))
        bank_pool = ctx.enter_context(tc.psum_pool(name="bank", bufs=4))
        ctx.enter_context(tc.manual_schedule())

        incidence_by_tile = incidence.rearrange("(p a) k -> p a k", a=NODE_TILES)
        features_by_tile = node_features.rearrange("(p a) c -> p a c", a=NODE_TILES)
        out_by_tile = out.rearrange("(p a) c -> p a c", a=NODE_TILES)

        identity = consts.tile([P, P], F32)
        make_identity(nc, identity[:])

        features = consts.tile([P, NODE_TILES, CHANNELS], BF16)

        ones = consts.tile([P, P], BF16)
        nc.vector.memset(ones[:], 1.0)
        bias_rows = consts.tile([P, CHANNELS], BF16)
        nc.vector.memset(bias_rows[:], 0.0)

        w2_codes = consts.tile([P, CHANNELS], U32, align_bytes=64)
        w2_scales = consts.tile([P, CHANNELS], U8, align_bytes=64)
        nc.vector.memset(w2_scales[:].bitcast(I32), 0)

        bias = consts.tile([P, CHANNELS], F32)

        def spread_bias():
            bias_bank = bank_pool.tile([P, CHANNELS], F32, name="bias_bank", tag="bank")
            nc.tensor.matmul(out=bias_bank[:], lhsT=ones[:], rhs=bias_rows[:], start=True, stop=True)
            nc.vector.tensor_copy(out=bias[:], in_=bias_bank[:])

        residual = consts.tile([P, NODE_TILES, CHANNELS], F32)

        def add_residual(a):
            nc.vector.tensor_tensor(out=residual[:, a, :], in0=bias[:], in1=features[:, a, :], op=ADD)

        acc = [acc_pool.tile([P, CHANNELS], F32, name="acc%d" % a) for a in range(NODE_TILES)]

        chunk_passes = {}
        chunk_first = {}
        for a in range(NODE_TILES):
            first = 0
            for passes in incidence_chunks(a):
                chunk_passes[first, a] = passes
                for g in range(first, first + passes):
                    chunk_first[g, a] = first
                first += passes

        inc_raw = {}
        he_raw = {}
        inc_grouped = {}
        he_grouped = {}
        inc_codes = {}
        inc_scales = {}
        he_codes = {}
        he_scales = {}

        def load_incidence(first):
            for a in range(NODE_TILES):
                if (first, a) in chunk_passes:
                    edges = chunk_passes[first, a] * K_PASS
                    inc_raw[first, a] = inc_pool.tile([P, edges], BF16, name="inc_raw")
                    nc.sync.dma_start(
                        out=inc_raw[first, a][:],
                        in_=incidence_by_tile[:, a, first * K_PASS : first * K_PASS + edges],
                    )

        def load_he(g):
            he_raw[g] = he_pool.tile([P, PACK, CHANNELS], BF16, name="he_raw")
            rows = he[g * K_PASS : (g + 1) * K_PASS, :]
            if g < LONG_ROW_PASSES:
                nc.sync.dma_start(
                    out=he_raw[g][:].rearrange("p t c -> p (t c)"),
                    in_=rows.rearrange("(p t) c -> p (t c)", t=PACK),
                )
            else:
                nc.sync.dma_start(
                    out=he_raw[g][:].rearrange("p (u e) c -> p u (e c)", u=2),
                    in_=rows.rearrange("(u p e) c -> p u (e c)", u=2, p=P),
                )

        def load_for(g):
            if g + INC_AHEAD < LAST and g + INC_AHEAD > 0:
                load_incidence(g + INC_AHEAD)
            if g == W2_AT:
                load_w2()
            if g == SMALL_AT:
                nc.sync.dma_start(out=bias_rows[0:1, :], in_=b2.unsqueeze(0))
                nc.sync.dma_start(out=features[:], in_=features_by_tile)
            if g >= 0:
                load_he(g)
            if g == LAST - LAST_BEFORE:
                load_incidence(LAST)
            if g == LAST and W2_AT > LAST:
                load_w2()

        def load_w2():
            nc.sync.dma_start(
                out=w2_codes[:].bitcast(I32),
                in_=W2_words[0].rearrange("p n t -> p (n t)").bitcast(I32),
            )
            for quadrant in range(4):
                nc.sync.dma_start(
                    out=w2_scales[32 * quadrant : 32 * quadrant + 4, :].bitcast(I32),
                    in_=W2_scales[0, 4 * quadrant : 4 * quadrant + 4, :].bitcast(I32),
                )

        xb = {}

        def transpose_incidence(g):
            inc_grouped[g] = grouped_pool.tile([P, PACK * NODES], BF16, name="inc_grouped", align_bytes=64)
            grouped_words = inc_grouped[g][:].bitcast(F32)
            for half in range(2):
                bank = bank_pool.tile([P, 2, 2 * P], F32, name="xt", tag="bank")
                for i in range(2):
                    a = 2 * half + i
                    words = inc_raw[chunk_first[g, a], a][:].bitcast(F32)
                    first_word = (g - chunk_first[g, a]) * PASS_WORDS
                    for u in range(2):
                        nc.tensor.transpose(
                            out=bank[:, u, i * P : (i + 1) * P],
                            in_=(
                                words[:, first_word + u : first_word + PASS_WORDS : 2]
                                if g < LONG_ROW_PASSES
                                else words[:, first_word + u * P : first_word + (u + 1) * P]
                            ),
                            identity=identity[:],
                        )
                xb[g, half] = bank

        def evac(g):
            grouped_words = inc_grouped[g][:].bitcast(F32)
            for half in range(2):
                bank = xb[g, half]
                nc.scalar.copy(
                    out=grouped_words[:, half * BANK_WORDS : (half + 1) * BANK_WORDS].rearrange(
                        "p (n u) -> p n u", u=2
                    ),
                    in_=bank[:].rearrange("p u n -> p n u"),
                )

        def quantise_incidence(g):
            inc_codes[g] = mx_pool.tile([P, NODES], U32, name="inc_codes", align_bytes=64)
            inc_scales[g] = mx_pool.tile([P, NODES], U8, name="inc_scales", align_bytes=64)
            nc.vector.quantize_mx(
                out=inc_codes[g][:].bitcast(FP8X4), scales=inc_scales[g][:], in_=inc_grouped[g][:]
            )

        rr = {}

        def regroup_he(g):
            if g in rr:
                return
            he_grouped[g] = grouped_pool.tile([P, PACK * CHANNELS], BF16, name="he_grouped", align_bytes=64)
            src = he_raw[g][:].rearrange("q j (c i) -> q c j i", i=GROUP)
            dst = he_grouped[g][:].rearrange("q (c i j) -> q c j i", i=GROUP, j=PACK)
            rr[g] = (dst, src, {LAST - 1: SPLIT30, LAST: SPLIT31}.get(g, VECTOR_GROUPS))

        def rv(g):
            regroup_he(g)
            dst, src, split = rr[g]
            nc.vector.tensor_copy(out=dst[:, 0:split], in_=src[:, 0:split])

        def rs(g):
            regroup_he(g)
            dst, src, split = rr[g]
            nc.scalar.copy(out=dst[:, split:CHANNEL_GROUPS], in_=src[:, split:CHANNEL_GROUPS])

        def quantise_he(g):
            he_codes[g] = mx_pool.tile([P, CHANNELS], U32, name="he_codes", align_bytes=64)
            he_scales[g] = mx_pool.tile([P, CHANNELS], U8, name="he_scales", align_bytes=64)
            nc.vector.quantize_mx(
                out=he_codes[g][:].bitcast(FP8X4), scales=he_scales[g][:], in_=he_grouped[g][:]
            )

        last_bank = {}
        last_grouped = {}
        last_codes = {}
        last_scales = {}

        def multiply_tile(g, a):
            if g == LAST:
                codes, scales = last_codes[a][:], last_scales[a][:]
            else:
                nodes = slice(a * P, (a + 1) * P)
                codes, scales = inc_codes[g][:, nodes], inc_scales[g][:, nodes]
            nc.tensor.matmul_mx(
                out=acc[a][:],
                lhsT=codes.bitcast(FP8X4),
                lhsT_scale=scales,
                rhs=he_codes[g][:].bitcast(FP8X4),
                rhs_scale=he_scales[g][:],
                start=(g == 0),
                stop=(g == LAST),
            )

        def multiply(g):
            for a in range(NODE_TILES):
                multiply_tile(g, a)

        prop_bf = {}
        prop_bank = {}
        prop_codes = {}
        prop_scales = {}

        def regroup_words(bank, name, vec=False):
            grouped = tail_pool.tile([P, PACK * P], BF16, name=name, align_bytes=64)
            dst = grouped[:].bitcast(F32).rearrange("p (n u) -> p n u", u=2)
            if vec:
                nc.vector.tensor_copy(out=dst, in_=bank[:].rearrange("p u n -> p n u"))
            else:
                nc.scalar.copy(out=dst, in_=bank[:].rearrange("p u n -> p n u"))
            return grouped

        def quantise_tile(grouped, name):
            codes = tail_pool.tile([P, P], U32, name=name + "_codes", align_bytes=64)
            scales = tail_pool.tile([P, P], U8, name=name + "_scales", align_bytes=64)
            nc.vector.quantize_mx(out=codes[:].bitcast(FP8X4), scales=scales[:], in_=grouped[:])
            return codes, scales

        def transpose_words(words, name):
            bank = bank_pool.tile([P, 2, P], F32, name=name, tag="bank")
            for u in range(2):
                nc.tensor.transpose(
                    out=bank[:, u, :], in_=words[:, u * P : (u + 1) * P], identity=identity[:]
                )
            return bank

        def finish_sums(a):
            prop_bf[a] = tail_pool.tile([P, CHANNELS], BF16, name="prop_bf")
            dst = prop_bf[a][:].rearrange("p (u w e) -> p u w e", u=2, e=2)
            src = acc[a][:].rearrange("p (w u e) -> p u w e", u=2, e=2)
            if a not in VEVAC:
                nc.scalar.copy(out=dst, in_=src)
            else:
                nc.vector.tensor_copy(out=dst, in_=src)

        def second_product(a):
            product = acc_pool.tile([P, CHANNELS], F32, name="acc%d" % a)
            nc.tensor.matmul_mx(
                out=product[:],
                lhsT=prop_codes[a][:].bitcast(FP8X4),
                lhsT_scale=prop_scales[a][:],
                rhs=w2_codes[:].bitcast(FP8X4),
                rhs_scale=w2_scales[:],
                start=True,
                stop=True,
            )
            result = tail_pool.tile([P, CHANNELS], F32, name="result")
            nc.vector.tensor_tensor(out=result[:], in0=product[:], in1=residual[:, a, :], op=ADD)
            nc.sync.dma_start(out=out_by_tile[:, a, :], in_=result[:])

        A, B, CC, DD, SEQ = 1, 0, 0, 1, "TsEviqM"

        def T(g):
            if g < LAST:
                transpose_incidence(g)
            else:
                for a in range(NODE_TILES):
                    last_bank[a] = transpose_words(inc_raw[LAST, a][:].bitcast(F32), "xt_last")

        def E(g):
            if g < LAST:
                evac(g)
            else:
                for a in range(NODE_TILES):
                    last_grouped[a] = regroup_words(last_bank[a], "last_grouped")

        def Q(g):
            if g < LAST:
                quantise_incidence(g)
            else:
                for a in range(NODE_TILES):
                    last_codes[a], last_scales[a] = quantise_tile(last_grouped[a], "last")

        def M(g):
            if g < LAST - HELD:
                multiply(g)
            if g == LAST:
                for a in range(NODE_TILES):
                    for h in range(LAST - HELD, PASSES):
                        multiply_tile(h, a)
                    finish_sums(a)

        load_incidence(0)
        for g in range(-1, HE_BUFS):
            load_for(g)
        for step in range(-A, PASSES + DD):
            for op in SEQ:
                f, g = {"T": (T, step + A), "E": (E, step + A), "i": (Q, step + B), "q": (quantise_he, step - CC), "v": (rv, step), "s": (rs, step), "M": (M, step - DD)}[op]
                if 0 <= g < (LAST if op in "TEi" else PASSES):
                    f(g)
                if op == "s" and step == LAST and TLAST:
                    T(LAST)
                    E(LAST)
            if step == LAST:
                if not TLAST:
                    T(LAST)
                    E(LAST)
                Q(LAST)
            if step == RESIDUAL_AT - 1:
                spread_bias()
            for a in RES.get(step, ()):
                add_residual(a)
            if 0 <= step and step + HE_BUFS < PASSES:
                load_for(step + HE_BUFS)

        for a in range(NODE_TILES + MLAG):
            if a < NODE_TILES:
                prop_bank[a] = transpose_words(prop_bf[a][:].bitcast(F32), "pt")
                grouped = regroup_words(prop_bank[a], "prop_grouped", a in VE2)
                prop_codes[a], prop_scales[a] = quantise_tile(grouped, "prop")
            if a >= MLAG:
                second_product(a - MLAG)
